import numpy as np
import ml_dtypes


def mxq(x, axis, fmt="e4m3"):
    dtype, down = {"e4m3": (ml_dtypes.float8_e4m3fn, 7), "e5m2": (ml_dtypes.float8_e5m2, 14)}[fmt]
    v = np.moveaxis(np.asarray(x, np.float32).astype(ml_dtypes.bfloat16).astype(np.float64), axis, -1)
    blocks = v.reshape(v.shape[:-1] + (-1, 32))
    amax = np.abs(blocks).max(-1, keepdims=True)
    byte = np.maximum(np.where(amax > 0, np.frexp(amax)[1] - 1 + 127, 0) - down, 1)
    scale = np.exp2(byte - 127.0)
    codes = (blocks / scale).astype(np.float32).astype(dtype).astype(np.float64)
    return np.moveaxis((codes * scale).reshape(v.shape), -1, axis)


WIDE = False


def mx_kscale(k):
    if not WIDE:
        return np.ones(k)
    levels = np.array([10, -10, 5, -5, 0])
    if k % 512:
        return np.exp2(np.random.permutation(np.resize(levels, k // 32))).repeat(32)
    a = np.empty((k // 512, 16))
    for p in range(k // 512):
        a[p, :8] = np.random.permutation(np.resize(levels, 8))
        for g in range(8):
            far = levels[np.abs(levels - a[p, g]) >= 10]
            a[p, g + 8] = far[np.random.randint(len(far))]
    return np.exp2(a.ravel()).repeat(32)


BF16 = ml_dtypes.bfloat16


def bf(x):
    return np.asarray(x, np.float32).astype(BF16)


def f64(x):
    return np.asarray(x).astype(np.float64)


E2M1 = np.array([0.0, 0.5, 1.0, 1.5, 2.0, 3.0, 4.0, 6.0, -0.0, -0.5, -1.0, -1.5, -2.0, -3.0, -4.0, -6.0])


def pack_weight(w, fmt):
    k, n = w.shape
    w = f64(bf(w)).reshape(k // 32, 32, n)
    amax = np.abs(w).max(1)
    if fmt == "e4m3":
        byte = np.frexp(amax)[1] - 1 + 127 - 7
    else:
        mant, ex = np.frexp(amax / 6.0)
        byte = np.where(mant > 0.5, ex, ex - 1) + 127
    byte = np.clip(np.where(amax > 0, byte, 1), 1, 254)
    scaled = (w * np.exp2(127.0 - byte)[:, None, :]).reshape(k, n).astype(np.float32)
    by_word = np.ascontiguousarray(scaled.reshape(k // 512, 128, 4, n).transpose(0, 1, 3, 2))
    if fmt == "e4m3":
        words = by_word.astype(ml_dtypes.float8_e4m3fn).view(np.uint8)
    else:
        c = by_word.astype(ml_dtypes.float4_e2m1fn).view(np.uint8) & 0xF
        words = c[..., 0::2] | (c[..., 1::2] << 4)
    return np.ascontiguousarray(words), np.ascontiguousarray(byte.astype(np.uint8).reshape(k // 512, 16, n))


def unpack_weight(words, scales, fmt):
    g, p, n, _ = words.shape
    if fmt == "e4m3":
        vals = np.ascontiguousarray(words).view(ml_dtypes.float8_e4m3fn).astype(np.float64)
    else:
        nib = np.empty((g, p, n, 4), np.uint8)
        nib[..., 0::2] = words & 0xF
        nib[..., 1::2] = words >> 4
        vals = E2M1[nib]
    vals = vals * np.repeat(np.exp2(scales.astype(np.float64) - 127.0), 8, axis=1)[..., None]
    return vals.transpose(0, 1, 3, 2).reshape(g * 512, n)


B, S, N, D = 2, 2, 1024, 512


def setup_inputs():
    s, t = mx_kscale(D), mx_kscale(D)
    tensor0 = bf(np.random.standard_normal((S, N, D)) * s)
    tensor1 = bf(np.random.standard_normal((S, N, D)) * 0.5 / t)
    kernel = np.random.standard_normal((D, D)) * D ** -0.75 * t[:, None] / s[None, :]
    words, scales = pack_weight(np.ascontiguousarray(kernel.T), "e4m3")
    bias = bf(0.5 + 0.1 * np.random.standard_normal(1))
    return {"tensor0": tensor0,
            "tensor1": tensor1,
            "kernel_words": words,
            "kernel_scales": scales,
            "bias": bias}


def reference(tensor0, tensor1, kernel_words, kernel_scales, bias):
    q = mxq(f64(tensor0), 2, "e4m3") @ unpack_weight(kernel_words, kernel_scales, "e4m3")
    out = mxq(f64(tensor1), 2, "e4m3") @ mxq(q, 2, "e4m3").transpose(0, 2, 1)
    out = out + f64(bias)
    return np.ascontiguousarray(np.broadcast_to(out[None], (B,) + out.shape))

@@ -1,0 +1,237 @@
+import concourse.mybir as mybir
+from concourse.masks import make_identity
+
+BF16 = mybir.dt.bfloat16
+F32 = mybir.dt.float32
+I32 = mybir.dt.int32
+U32 = mybir.dt.uint32
+U8 = mybir.dt.uint8
+FP8X4 = mybir.dt.float8_e4m3fn_x4
+IDENTITY = mybir.ActivationFunctionType.Identity
+
+S = 2
+COPIES = 2
+ROWS = 1024
+D = 512
+P = 128
+PACK = 4
+BANK = 512
+
+STEPS = 4
+STEP_ROWS = ROWS // STEPS
+T0_FOLD = STEP_ROWS // P
+T1_FOLD = ROWS // P
+T1_STEP = T1_FOLD // STEPS
+
+WARM_UP = 6
+
+FLOPS = 2 * S * ROWS * D * D + 2 * S * ROWS * ROWS * D
+
+
+def tile_bilinear_kernel(tc, tensor0, tensor1, kernel_words, kernel_scales, bias, out):
+    nc = tc.nc
+    with (
+        tc.tile_pool(name="constants", bufs=1) as constants,
+        tc.tile_pool(name="inputs", bufs=1) as inputs,
+        tc.tile_pool(name="operands", bufs=1) as operands,
+        tc.tile_pool(name="results", bufs=S * STEPS) as results,
+        tc.psum_pool(name="psum_transposed", bufs=3) as psum_transposed,
+        tc.psum_pool(name="psum_sums", bufs=4) as psum_sums,
+        tc.psum_pool(name="psum_unread", bufs=1) as psum_unread,
+        tc.manual_schedule(),
+    ):
+        ident_f32 = constants.tile([P, P], F32)
+        bias_bf16 = constants.tile([P, 1], BF16)
+        bias_f32 = constants.tile([P, 1], F32)
+        table_warmer = constants.tile([P, 1], F32)
+        zeros = constants.tile([P, BANK], BF16)
+        w_codes_raw = constants.tile([P, D], U32, align_bytes=64)
+        w_scales_raw = constants.tile([P, D], U8, align_bytes=64)
+        w_codes = constants.tile([P, D], U32, align_bytes=64)
+        w_scales = constants.tile([P, D], U8, align_bytes=64)
+        t0_raw = [inputs.tile([P, STEPS, T0_FOLD, D], BF16, name="t0_raw%d" % s) for s in range(S)]
+        t1_raw = [inputs.tile([P, T1_FOLD, D], BF16, name="t1_raw%d" % s) for s in range(S)]
+
+        t0_grouped = operands.tile([P, ROWS, PACK], BF16, align_bytes=64)
+        q_grouped = operands.tile([P, ROWS, PACK], BF16, align_bytes=64)
+        t1_grouped = operands.tile([P, ROWS, PACK], BF16, align_bytes=64)
+
+        def mx_operand(name):
+            codes = [operands.tile([P, ROWS], U32, name="%s_codes%d" % (name, s), align_bytes=64) for s in range(S)]
+            scales = [operands.tile([P, ROWS], U8, name="%s_scales%d" % (name, s), align_bytes=64) for s in range(S)]
+            return codes, scales
+
+        t0_codes, t0_scales = mx_operand("t0")
+        q_codes, q_scales = mx_operand("q")
+        t1_codes, t1_scales = mx_operand("t1")
+
+        def step_cols(a):
+            return slice(STEP_ROWS * a, STEP_ROWS * (a + 1))
+
+        def load_t0(s, a):
+            nc.sync.dma_start(
+                out=t0_raw[s][:, a], in_=tensor0[s, step_cols(a), :].rearrange("(p h) e -> p h e", h=T0_FOLD)
+            )
+
+        def load_t1(s):
+            nc.sync.dma_start(out=t1_raw[s][:], in_=tensor1[s].rearrange("(p r) d -> p r d", r=T1_FOLD))
+
+        def load_w():
+            for quadrant in range(4):
+                nc.sync.dma_start(
+                    out=w_scales_raw[32 * quadrant : 32 * quadrant + 4, :].bitcast(I32),
+                    in_=kernel_scales[0, 4 * quadrant : 4 * quadrant + 4, :].bitcast(I32),
+                )
+            nc.sync.dma_start(
+                out=w_codes_raw[:].bitcast(I32),
+                in_=kernel_words[0].rearrange("p n t -> p (n t)").bitcast(I32),
+            )
+
+        nc.vector.memset(zeros[:], 0.0)
+        nc.vector.memset(w_scales_raw[:].bitcast(I32), 0)
+        nc.vector.memset(table_warmer[:], 0.0)
+        nc.scalar.dma_start(out=bias_bf16[:], in_=bias.partition_broadcast(P))
+        load_t0(0, 0)
+        load_t0(0, 1)
+        load_w()
+        load_t0(0, 2)
+        load_t0(0, 3)
+        load_t1(0)
+        for a in range(STEPS):
+            load_t0(1, a)
+        load_t1(1)
+
+        def keep_tensor_engine_busy(count):
+            unread = psum_unread.tile([P, BANK], F32)
+            for i in range(count):
+                nc.tensor.matmul(out=unread[:], lhsT=zeros[:, 0:P], rhs=zeros[:], start=(i == 0), stop=(i == count - 1))
+
+        keep_tensor_engine_busy(WARM_UP)
+
+        nc.scalar.activation(out=table_warmer[:], in_=table_warmer[:], func=IDENTITY)
+
+        make_identity(nc, ident_f32[:])
+        nc.gpsimd.tensor_copy(out=bias_f32[:], in_=bias_bf16[:])
+
+        nc.vector.tensor_copy(
+            out=w_codes[:].bitcast(I32).rearrange("p (t m) -> p t m", t=PACK),
+            in_=w_codes_raw[:].bitcast(I32).rearrange("p (m t) -> p t m", t=PACK),
+        )
+        nc.vector.tensor_copy(
+            out=w_scales[:].rearrange("p (t m) -> p t m", t=PACK),
+            in_=w_scales_raw[:].rearrange("p (m t) -> p t m", t=PACK),
+        )
+
+        def transpose_t0(s, a):
+            words = t0_raw[s][:, a].bitcast(F32)
+            t0_t = psum_transposed.tile([P, T0_FOLD, 2, P], F32, tag="transposed")
+            for h in range(T0_FOLD):
+                for u in range(2):
+                    nc.tensor.transpose(t0_t[:, h, u, :], words[:, h, u : D // 2 : 2], ident_f32[:])
+            keep_tensor_engine_busy(1)
+            nc.scalar.copy(
+                out=t0_grouped[:, step_cols(a), :].bitcast(F32).rearrange("p (c h) u -> p c h u", h=T0_FOLD),
+                in_=t0_t[:].rearrange("p h u c -> p c h u"),
+            )
+
+        def quantise_t0(s, a):
+            nc.vector.quantize_mx(
+                out=t0_codes[s][:, step_cols(a)].bitcast(FP8X4),
+                scales=t0_scales[s][:, step_cols(a)],
+                in_=t0_grouped[:, step_cols(a), :].rearrange("p j t -> p (j t)"),
+            )
+
+        def multiply_by_w(s, a):
+            for block in range(STEP_ROWS // P):
+                j_cols = slice(STEP_ROWS * a + P * block, STEP_ROWS * a + P * (block + 1))
+                q_t = psum_sums.tile([P, PACK, P], F32, tag="sums")
+                for t in range(PACK):
+                    d_cols = slice(P * t, P * (t + 1))
+                    nc.tensor.matmul_mx(
+                        out=q_t[:, t, :],
+                        lhsT=w_codes[:, d_cols].bitcast(FP8X4),
+                        lhsT_scale=w_scales[:, d_cols],
+                        rhs=t0_codes[s][:, j_cols].bitcast(FP8X4),
+                        rhs_scale=t0_scales[s][:, j_cols],
+                        start=True,
+                        stop=True,
+                    )
+                copy = nc.vector.tensor_copy if block % 2 == 0 else nc.scalar.copy
+                copy(out=q_grouped[:, j_cols, :], in_=q_t[:].rearrange("p t j -> p j t"))
+
+        def quantise_q(s, a):
+            nc.vector.quantize_mx(
+                out=q_codes[s][:, step_cols(a)].bitcast(FP8X4),
+                scales=q_scales[s][:, step_cols(a)],
+                in_=q_grouped[:, step_cols(a), :].rearrange("p j t -> p (j t)"),
+            )
+
+        def transpose_t1(s, a):
+            words = t1_raw[s][:].bitcast(F32)
+            for r in range(T1_STEP * a, T1_STEP * (a + 1)):
+                t1_t = psum_transposed.tile([P, 2, P], F32, tag="transposed")
+                for u in range(2):
+                    nc.tensor.transpose(t1_t[:, u, :], words[:, r, u : D // 2 : 2], ident_f32[:])
+                copy = nc.vector.tensor_copy if r % 2 == 0 else nc.scalar.copy
+                copy(
+                    out=t1_grouped[:, P * r : P * (r + 1), :].bitcast(F32),
+                    in_=t1_t[:].rearrange("p u c -> p c u"),
+                )
+
+        def quantise_t1(s, a):
+            nc.vector.quantize_mx(
+                out=t1_codes[s][:, step_cols(a)].bitcast(FP8X4),
+                scales=t1_scales[s][:, step_cols(a)],
+                in_=t1_grouped[:, step_cols(a), :].rearrange("p i t -> p (i t)"),
+            )
+
+        def multiply_and_store(s, a):
+            result = results.tile([P, T1_STEP, ROWS], F32)
+            for r in range(T1_STEP):
+                i_cols = slice(STEP_ROWS * a + P * r, STEP_ROWS * a + P * (r + 1))
+                for half in range(ROWS // BANK):
+                    j_cols = slice(BANK * half, BANK * (half + 1))
+                    score = psum_sums.tile([P, BANK], F32, tag="sums")
+                    nc.tensor.matmul_mx(
+                        out=score[:],
+                        lhsT=t1_codes[s][:, i_cols].bitcast(FP8X4),
+                        lhsT_scale=t1_scales[s][:, i_cols],
+                        rhs=q_codes[s][:, j_cols].bitcast(FP8X4),
+                        rhs_scale=q_scales[s][:, j_cols],
+                        start=True,
+                        stop=True,
+                    )
+                    if half == 0:
+                        nc.vector.tensor_scalar(
+                            out=result[:, r, j_cols],
+                            in0=score[:],
+                            scalar1=bias_f32[:, 0:1],
+                            scalar2=None,
+                            op0=mybir.AluOpType.add,
+                        )
+                    else:
+                        nc.scalar.activation(out=result[:, r, j_cols], in_=score[:], func=IDENTITY, bias=bias_f32[:, 0:1])
+            for b in range(COPIES):
+                rows = out[b, s].rearrange("(p r) j -> p r j", r=T1_FOLD)
+                nc.sync.dma_start(out=rows[:, T1_STEP * a : T1_STEP * (a + 1), :], in_=result[:])
+
+        for s in range(S):
+            for tick in range(STEPS + 3):
+                if tick < STEPS:
+                    transpose_t0(s, tick)
+                if tick == STEPS:
+                    transpose_t1(s, 0)
+                if 0 <= tick - 1 < STEPS:
+                    quantise_t0(s, tick - 1)
+                if 0 <= tick - 2 < STEPS:
+                    multiply_by_w(s, tick - 2)
+                if tick - 1 == STEPS:
+                    quantise_t1(s, 0)
+                if 0 <= tick - 3 < STEPS:
+                    quantise_q(s, tick - 3)
+            for a in range(STEPS):
+                if a + 1 < STEPS:
+                    transpose_t1(s, a + 1)
+                multiply_and_store(s, a)
+                if a + 1 < STEPS:
+                    quantise_t1(s, a + 1)

@@ -19,7 +19,9 @@ BANK = 512
 
 STEPS = 4
 STEP_ROWS = ROWS // STEPS
-T0_FOLD = STEP_ROWS // P
+HALVES = ROWS // BANK
+HALF_FOLD = BANK // P
+UNIT_STEP = STEP_ROWS // P
 T1_FOLD = ROWS // P
 T1_STEP = T1_FOLD // STEPS
 
@@ -34,10 +36,9 @@ def tile_bilinear_kernel(tc, tensor0, tensor1, kernel_words, kernel_scales, bias
         tc.tile_pool(name="constants", bufs=1) as constants,
         tc.tile_pool(name="inputs", bufs=1) as inputs,
         tc.tile_pool(name="operands", bufs=1) as operands,
-        tc.tile_pool(name="results", bufs=S * STEPS) as results,
-        tc.psum_pool(name="psum_transposed", bufs=3) as psum_transposed,
+        tc.tile_pool(name="results", bufs=1) as results,
+        tc.psum_pool(name="psum_transposed", bufs=4) as psum_transposed,
         tc.psum_pool(name="psum_sums", bufs=4) as psum_sums,
-        tc.psum_pool(name="psum_unread", bufs=1) as psum_unread,
         tc.manual_schedule(),
     ):
         ident_f32 = constants.tile([P, P], F32)
@@ -49,7 +50,7 @@ def tile_bilinear_kernel(tc, tensor0, tensor1, kernel_words, kernel_scales, bias
         w_scales_raw = constants.tile([P, D], U8, align_bytes=64)
         w_codes = constants.tile([P, D], U32, align_bytes=64)
         w_scales = constants.tile([P, D], U8, align_bytes=64)
-        t0_raw = [inputs.tile([P, STEPS, T0_FOLD, D], BF16, name="t0_raw%d" % s) for s in range(S)]
+        t0_raw = [inputs.tile([P, HALVES, HALF_FOLD, D], BF16, name="t0_raw%d" % s) for s in range(S)]
         t1_raw = [inputs.tile([P, T1_FOLD, D], BF16, name="t1_raw%d" % s) for s in range(S)]
 
         t0_grouped = operands.tile([P, ROWS, PACK], BF16, align_bytes=64)
@@ -68,41 +69,41 @@ def tile_bilinear_kernel(tc, tensor0, tensor1, kernel_words, kernel_scales, bias
         def step_cols(a):
             return slice(STEP_ROWS * a, STEP_ROWS * (a + 1))
 
-        def load_t0(s, a):
-            nc.sync.dma_start(
-                out=t0_raw[s][:, a], in_=tensor0[s, step_cols(a), :].rearrange("(p h) e -> p h e", h=T0_FOLD)
-            )
+        def load_t0(s, half, h0, count):
+            rows = tensor0[s, BANK * half : BANK * (half + 1), :].rearrange("(p h) e -> p h e", h=HALF_FOLD)
+            nc.sync.dma_start(out=t0_raw[s][:, half, h0 : h0 + count], in_=rows[:, h0 : h0 + count])
 
         def load_t1(s):
             nc.sync.dma_start(out=t1_raw[s][:], in_=tensor1[s].rearrange("(p r) d -> p r d", r=T1_FOLD))
 
-        def load_w():
+        def load_w_scales():
             for quadrant in range(4):
                 nc.sync.dma_start(
                     out=w_scales_raw[32 * quadrant : 32 * quadrant + 4, :].bitcast(I32),
                     in_=kernel_scales[0, 4 * quadrant : 4 * quadrant + 4, :].bitcast(I32),
                 )
+
+        def load_w_codes():
             nc.sync.dma_start(
                 out=w_codes_raw[:].bitcast(I32),
                 in_=kernel_words[0].rearrange("p n t -> p (n t)").bitcast(I32),
             )
 
-        nc.vector.memset(zeros[:], 0.0)
         nc.vector.memset(w_scales_raw[:].bitcast(I32), 0)
+        nc.vector.memset(zeros[:], 0.0)
         nc.vector.memset(table_warmer[:], 0.0)
-        nc.scalar.dma_start(out=bias_bf16[:], in_=bias.partition_broadcast(P))
-        load_t0(0, 0)
-        load_t0(0, 1)
-        load_w()
-        load_t0(0, 2)
-        load_t0(0, 3)
+        load_t0(0, 0, 0, UNIT_STEP)
+        load_w_scales()
+        load_w_codes()
+        load_t0(0, 0, UNIT_STEP, UNIT_STEP)
         load_t1(0)
-        for a in range(STEPS):
-            load_t0(1, a)
+        load_t0(0, 1, 0, HALF_FOLD)
+        for half in range(HALVES):
+            load_t0(1, half, 0, HALF_FOLD)
         load_t1(1)
 
         def keep_tensor_engine_busy(count):
-            unread = psum_unread.tile([P, BANK], F32)
+            unread = psum_sums.tile([P, BANK], F32, tag="sums")
             for i in range(count):
                 nc.tensor.matmul(out=unread[:], lhsT=zeros[:, 0:P], rhs=zeros[:], start=(i == 0), stop=(i == count - 1))
 
@@ -110,29 +111,50 @@ def tile_bilinear_kernel(tc, tensor0, tensor1, kernel_words, kernel_scales, bias
 
         nc.scalar.activation(out=table_warmer[:], in_=table_warmer[:], func=IDENTITY)
 
+        nc.gpsimd.dma_start(out=bias_bf16[:], in_=bias.partition_broadcast(P))
         make_identity(nc, ident_f32[:])
         nc.gpsimd.tensor_copy(out=bias_f32[:], in_=bias_bf16[:])
 
-        nc.vector.tensor_copy(
-            out=w_codes[:].bitcast(I32).rearrange("p (t m) -> p t m", t=PACK),
-            in_=w_codes_raw[:].bitcast(I32).rearrange("p (m t) -> p t m", t=PACK),
-        )
-        nc.vector.tensor_copy(
-            out=w_scales[:].rearrange("p (t m) -> p t m", t=PACK),
-            in_=w_scales_raw[:].rearrange("p (m t) -> p t m", t=PACK),
-        )
-
-        def transpose_t0(s, a):
-            words = t0_raw[s][:, a].bitcast(F32)
-            t0_t = psum_transposed.tile([P, T0_FOLD, 2, P], F32, tag="transposed")
-            for h in range(T0_FOLD):
-                for u in range(2):
-                    nc.tensor.transpose(t0_t[:, h, u, :], words[:, h, u : D // 2 : 2], ident_f32[:])
-            keep_tensor_engine_busy(1)
-            nc.scalar.copy(
-                out=t0_grouped[:, step_cols(a), :].bitcast(F32).rearrange("p (c h) u -> p c h u", h=T0_FOLD),
-                in_=t0_t[:].rearrange("p h u c -> p c h u"),
+        def reorder(out, in_):
+            nc.vector.tensor_copy(
+                out=out.rearrange("p (t m) -> p t m", t=PACK), in_=in_.rearrange("p (m t) -> p t m", t=PACK)
             )
+
+        def reorder_w_scales():
+            reorder(w_scales[:], w_scales_raw[:])
+
+        def reorder_w_codes():
+            reorder(w_codes[:].bitcast(I32), w_codes_raw[:].bitcast(I32))
+
+        def copy_out(engine, out, in_):
+            if engine == "V":
+                nc.vector.tensor_copy(out=out, in_=in_)
+            else:
+                nc.scalar.copy(out=out, in_=in_)
+
+        def unit_cols(u):
+            return slice(P * u, P * (u + 1))
+
+        def transpose_words(columns, words, count, engine):
+            turned = psum_transposed.tile([P, count, 2, P], F32, tag="transposed")
+            for i in range(count):
+                for u in range(2):
+                    nc.tensor.transpose(turned[:, i, u, :], words[:, i, u : D // 2 : 2], ident_f32[:])
+            copy_out(
+                engine,
+                columns.bitcast(F32).rearrange("p (i c) u -> p i c u", i=count),
+                turned[:].rearrange("p i u c -> p i c u"),
+            )
+
+        def transpose_step(raw, grouped, a, engines):
+            words = raw.bitcast(F32)
+            count = UNIT_STEP // len(engines)
+            for i, engine in enumerate(engines):
+                u = UNIT_STEP * a + count * i
+                transpose_words(grouped[:, P * u : P * (u + count), :], words[:, u : u + count, :], count, engine)
+
+        def transpose_t0(s, a, engines):
+            transpose_step(t0_raw[s][:].rearrange("p f h e -> p (f h) e"), t0_grouped, a, engines)
 
         def quantise_t0(s, a):
             nc.vector.quantize_mx(
@@ -141,23 +163,21 @@ def tile_bilinear_kernel(tc, tensor0, tensor1, kernel_words, kernel_scales, bias
                 in_=t0_grouped[:, step_cols(a), :].rearrange("p j t -> p (j t)"),
             )
 
-        def multiply_by_w(s, a):
-            for block in range(STEP_ROWS // P):
-                j_cols = slice(STEP_ROWS * a + P * block, STEP_ROWS * a + P * (block + 1))
-                q_t = psum_sums.tile([P, PACK, P], F32, tag="sums")
-                for t in range(PACK):
-                    d_cols = slice(P * t, P * (t + 1))
-                    nc.tensor.matmul_mx(
-                        out=q_t[:, t, :],
-                        lhsT=w_codes[:, d_cols].bitcast(FP8X4),
-                        lhsT_scale=w_scales[:, d_cols],
-                        rhs=t0_codes[s][:, j_cols].bitcast(FP8X4),
-                        rhs_scale=t0_scales[s][:, j_cols],
-                        start=True,
-                        stop=True,
-                    )
-                copy = nc.vector.tensor_copy if block % 2 == 0 else nc.scalar.copy
-                copy(out=q_grouped[:, j_cols, :], in_=q_t[:].rearrange("p t j -> p j t"))
+        def multiply_by_w(s, u, engine):
+            j_cols = unit_cols(u)
+            q_t = psum_sums.tile([P, PACK, P], F32, tag="sums")
+            for t in range(PACK):
+                d_cols = slice(P * t, P * (t + 1))
+                nc.tensor.matmul_mx(
+                    out=q_t[:, t, :],
+                    lhsT=w_codes[:, d_cols].bitcast(FP8X4),
+                    lhsT_scale=w_scales[:, d_cols],
+                    rhs=t0_codes[s][:, j_cols].bitcast(FP8X4),
+                    rhs_scale=t0_scales[s][:, j_cols],
+                    start=True,
+                    stop=True,
+                )
+            copy_out(engine, q_grouped[:, j_cols, :], q_t[:].rearrange("p t j -> p j t"))
 
         def quantise_q(s, a):
             nc.vector.quantize_mx(
@@ -166,17 +186,8 @@ def tile_bilinear_kernel(tc, tensor0, tensor1, kernel_words, kernel_scales, bias
                 in_=q_grouped[:, step_cols(a), :].rearrange("p j t -> p (j t)"),
             )
 
-        def transpose_t1(s, a):
-            words = t1_raw[s][:].bitcast(F32)
-            for r in range(T1_STEP * a, T1_STEP * (a + 1)):
-                t1_t = psum_transposed.tile([P, 2, P], F32, tag="transposed")
-                for u in range(2):
-                    nc.tensor.transpose(t1_t[:, u, :], words[:, r, u : D // 2 : 2], ident_f32[:])
-                copy = nc.vector.tensor_copy if r % 2 == 0 else nc.scalar.copy
-                copy(
-                    out=t1_grouped[:, P * r : P * (r + 1), :].bitcast(F32),
-                    in_=t1_t[:].rearrange("p u c -> p c u"),
-                )
+        def transpose_t1(s, a, engines):
+            transpose_step(t1_raw[s][:], t1_grouped, a, engines)
 
         def quantise_t1(s, a):
             nc.vector.quantize_mx(
@@ -185,53 +196,134 @@ def tile_bilinear_kernel(tc, tensor0, tensor1, kernel_words, kernel_scales, bias
                 in_=t1_grouped[:, step_cols(a), :].rearrange("p i t -> p (i t)"),
             )
 
-        def multiply_and_store(s, a):
-            result = results.tile([P, T1_STEP, ROWS], F32)
-            for r in range(T1_STEP):
-                i_cols = slice(STEP_ROWS * a + P * r, STEP_ROWS * a + P * (r + 1))
-                for half in range(ROWS // BANK):
-                    j_cols = slice(BANK * half, BANK * (half + 1))
-                    score = psum_sums.tile([P, BANK], F32, tag="sums")
-                    nc.tensor.matmul_mx(
-                        out=score[:],
-                        lhsT=t1_codes[s][:, i_cols].bitcast(FP8X4),
-                        lhsT_scale=t1_scales[s][:, i_cols],
-                        rhs=q_codes[s][:, j_cols].bitcast(FP8X4),
-                        rhs_scale=q_scales[s][:, j_cols],
-                        start=True,
-                        stop=True,
-                    )
-                    if half == 0:
-                        nc.vector.tensor_scalar(
-                            out=result[:, r, j_cols],
-                            in0=score[:],
-                            scalar1=bias_f32[:, 0:1],
-                            scalar2=None,
-                            op0=mybir.AluOpType.add,
-                        )
-                    else:
-                        nc.scalar.activation(out=result[:, r, j_cols], in_=score[:], func=IDENTITY, bias=bias_f32[:, 0:1])
+        def half_score(s, r, half, result, engine):
+            i_cols = unit_cols(r)
+            j_cols = slice(BANK * half, BANK * (half + 1))
+            score = psum_sums.tile([P, HALF_FOLD, P], F32, tag="sums")
+            nc.tensor.matmul_mx(
+                out=score[:].rearrange("p h c -> p (h c)"),
+                lhsT=t1_codes[s][:, i_cols].bitcast(FP8X4),
+                lhsT_scale=t1_scales[s][:, i_cols],
+                rhs=q_codes[s][:, j_cols].bitcast(FP8X4),
+                rhs_scale=q_scales[s][:, j_cols],
+                start=True,
+                stop=True,
+            )
+            out_half = result.rearrange("p (c h) -> p c h", h=HALF_FOLD)
+            score_in_order = score[:].rearrange("p h c -> p c h")
+            if engine == "V":
+                nc.vector.tensor_scalar(
+                    out=out_half, in0=score_in_order, scalar1=bias_f32[:, 0:1], scalar2=None, op0=mybir.AluOpType.add
+                )
+            else:
+                nc.scalar.activation(out=out_half, in_=score_in_order, func=IDENTITY, bias=bias_f32[:, 0:1])
+
+        def store(s, r0, count, j_cols, values):
             for b in range(COPIES):
                 rows = out[b, s].rearrange("(p r) j -> p r j", r=T1_FOLD)
-                nc.sync.dma_start(out=rows[:, T1_STEP * a : T1_STEP * (a + 1), :], in_=result[:])
+                nc.sync.dma_start(out=rows[:, r0 : r0 + count, j_cols], in_=values)
 
-        for s in range(S):
-            for tick in range(STEPS + 3):
-                if tick < STEPS:
-                    transpose_t0(s, tick)
-                if tick == STEPS:
-                    transpose_t1(s, 0)
-                if 0 <= tick - 1 < STEPS:
-                    quantise_t0(s, tick - 1)
-                if 0 <= tick - 2 < STEPS:
-                    multiply_by_w(s, tick - 2)
-                if tick - 1 == STEPS:
-                    quantise_t1(s, 0)
-                if 0 <= tick - 3 < STEPS:
-                    quantise_q(s, tick - 3)
-            for a in range(STEPS):
-                if a + 1 < STEPS:
-                    transpose_t1(s, a + 1)
-                multiply_and_store(s, a)
-                if a + 1 < STEPS:
-                    quantise_t1(s, a + 1)
+        def results_of(name, count, columns):
+            return results.tile([P, count, columns], F32, name="result_" + name)
+
+        left = slice(0, BANK)
+        right = slice(BANK, ROWS)
+        whole = slice(0, ROWS)
+
+        def half_scores(a, half, name):
+            result = results_of(name, T1_STEP, BANK)
+            for i, engine in enumerate("SV"):
+                half_score(0, T1_STEP * a + i, half, result[:, i, :], engine)
+            store(0, T1_STEP * a, T1_STEP, (left, right)[half], result[:])
+
+        def row_scores(s, r, result_row):
+            half_score(s, r, 0, result_row[:, left], "V")
+            half_score(s, r, 1, result_row[:, right], "S")
+
+        reorder_w_scales()
+        transpose_t0(0, 0, "VS")
+        reorder_w_codes()
+        quantise_t0(0, 0)
+        transpose_t0(0, 1, "SV")
+        multiply_by_w(0, 0, "S")
+        quantise_t0(0, 1)
+        multiply_by_w(0, 1, "V")
+        multiply_by_w(0, 2, "S")
+        quantise_q(0, 0)
+        multiply_by_w(0, 3, "V")
+        transpose_t1(0, 0, "SS")
+        quantise_q(0, 1)
+        quantise_t1(0, 0)
+        transpose_t0(0, 2, "SS")
+        half_scores(0, 0, "left0")
+        transpose_t0(0, 3, "SV")
+        quantise_t0(0, 2)
+        transpose_t1(0, 1, "SV")
+        multiply_by_w(0, 4, "S")
+        quantise_t0(0, 3)
+        quantise_t1(0, 1)
+        multiply_by_w(0, 5, "V")
+        half_scores(1, 0, "left1")
+        multiply_by_w(0, 6, "S")
+        quantise_q(0, 2)
+        multiply_by_w(0, 7, "V")
+        transpose_t1(0, 2, "S")
+        quantise_q(0, 3)
+        half_scores(0, 1, "right0")
+        quantise_t1(0, 2)
+        half_scores(1, 1, "right1")
+        transpose_t1(0, 3, "S")
+
+        def rows_and_store(s, r0, count):
+            result = results_of("%d_%d" % (s, r0), count, ROWS)
+            for r in range(count):
+                row_scores(s, r0 + r, result[:, r, :])
+            store(s, r0, count, whole, result[:])
+
+        middle = results_of("0_4", 2, ROWS)
+        last = results_of("0_6", 2, ROWS)
+        transpose_t0(1, 0, "S")
+        row_scores(0, 4, middle[:, 0, :])
+        quantise_t1(0, 3)
+        quantise_t0(1, 0)
+        row_scores(0, 5, middle[:, 1, :])
+        store(0, 4, 2, whole, middle[:])
+        transpose_t0(1, 1, "S")
+        multiply_by_w(1, 0, "V")
+        quantise_t0(1, 1)
+        multiply_by_w(1, 1, "S")
+        transpose_t0(1, 2, "S")
+        quantise_q(1, 0)
+        quantise_t0(1, 2)
+        multiply_by_w(1, 2, "V")
+        multiply_by_w(1, 3, "S")
+        row_scores(0, 6, last[:, 0, :])
+        transpose_t0(1, 3, "S")
+        quantise_q(1, 1)
+        quantise_t0(1, 3)
+        multiply_by_w(1, 4, "V")
+        multiply_by_w(1, 5, "S")
+        row_scores(0, 7, last[:, 1, :])
+        store(0, 6, 2, whole, last[:])
+        transpose_t1(1, 0, "S")
+        quantise_q(1, 2)
+        quantise_t1(1, 0)
+        multiply_by_w(1, 6, "V")
+        multiply_by_w(1, 7, "S")
+        transpose_t1(1, 1, "S")
+        quantise_q(1, 3)
+        quantise_t1(1, 1)
+
+        first = results_of("1_0", 2, ROWS)
+        row_scores(1, 0, first[:, 0, :])
+        transpose_t1(1, 2, "S")
+        row_scores(1, 1, first[:, 1, :])
+        store(1, 0, 2, whole, first[:])
+        quantise_t1(1, 2)
+        second = results_of("1_2", 2, ROWS)
+        row_scores(1, 2, second[:, 0, :])
+        transpose_t1(1, 3, "S")
+        row_scores(1, 3, second[:, 1, :])
+        store(1, 2, 2, whole, second[:])
+        quantise_t1(1, 3)
+        rows_and_store(1, 4, 4)

@@ -242,6 +242,7 @@ def tile_bilinear_kernel(tc, tensor0, tensor1, kernel_words, kernel_scales, bias
 
         reorder_w_scales()
         transpose_t0(0, 0, "VS")
+        keep_tensor_engine_busy(2)
         reorder_w_codes()
         quantise_t0(0, 0)
         transpose_t0(0, 1, "SV")
@@ -255,10 +256,12 @@ def tile_bilinear_kernel(tc, tensor0, tensor1, kernel_words, kernel_scales, bias
         quantise_q(0, 1)
         quantise_t1(0, 0)
         transpose_t0(0, 2, "SS")
+        keep_tensor_engine_busy(2)
         half_scores(0, 0, "left0")
         transpose_t0(0, 3, "SV")
         quantise_t0(0, 2)
         transpose_t1(0, 1, "SV")
+        keep_tensor_engine_busy(1)
         multiply_by_w(0, 4, "S")
         quantise_t0(0, 3)
         quantise_t1(0, 1)
@@ -268,6 +271,7 @@ def tile_bilinear_kernel(tc, tensor0, tensor1, kernel_words, kernel_scales, bias
         quantise_q(0, 2)
         multiply_by_w(0, 7, "V")
         transpose_t1(0, 2, "S")
+        keep_tensor_engine_busy(3)
         quantise_q(0, 3)
         half_scores(0, 1, "right0")
         quantise_t1(0, 2)
@@ -289,6 +293,7 @@ def tile_bilinear_kernel(tc, tensor0, tensor1, kernel_words, kernel_scales, bias
         row_scores(0, 5, middle[:, 1, :])
         store(0, 4, 2, whole, middle[:])
         transpose_t0(1, 1, "S")
+        keep_tensor_engine_busy(1)
         multiply_by_w(1, 0, "V")
         quantise_t0(1, 1)
         multiply_by_w(1, 1, "S")
@@ -311,6 +316,7 @@ def tile_bilinear_kernel(tc, tensor0, tensor1, kernel_words, kernel_scales, bias
         multiply_by_w(1, 6, "V")
         multiply_by_w(1, 7, "S")
         transpose_t1(1, 1, "S")
+        keep_tensor_engine_busy(3)
         quantise_q(1, 3)
         quantise_t1(1, 1)
 

@@ -93,9 +93,9 @@ def tile_bilinear_kernel(tc, tensor0, tensor1, kernel_words, kernel_scales, bias
         nc.vector.memset(zeros[:], 0.0)
         nc.vector.memset(table_warmer[:], 0.0)
         load_t0(0, 0, 0, UNIT_STEP)
+        load_t0(0, 0, UNIT_STEP, UNIT_STEP)
         load_w_scales()
         load_w_codes()
-        load_t0(0, 0, UNIT_STEP, UNIT_STEP)
         load_t1(0)
         load_t0(0, 1, 0, HALF_FOLD)
         for half in range(HALVES):
@@ -230,9 +230,9 @@ def tile_bilinear_kernel(tc, tensor0, tensor1, kernel_words, kernel_scales, bias
         right = slice(BANK, ROWS)
         whole = slice(0, ROWS)
 
-        def half_scores(a, half, name):
+        def half_scores(a, half, name, engines):
             result = results_of(name, T1_STEP, BANK)
-            for i, engine in enumerate("SV"):
+            for i, engine in enumerate(engines):
                 half_score(0, T1_STEP * a + i, half, result[:, i, :], engine)
             store(0, T1_STEP * a, T1_STEP, (left, right)[half], result[:])
 
@@ -240,43 +240,44 @@ def tile_bilinear_kernel(tc, tensor0, tensor1, kernel_words, kernel_scales, bias
             half_score(s, r, 0, result_row[:, left], "V")
             half_score(s, r, 1, result_row[:, right], "S")
 
+        transpose_t0(0, 0, "SS")
         reorder_w_scales()
-        transpose_t0(0, 0, "VS")
-        keep_tensor_engine_busy(2)
-        reorder_w_codes()
+        keep_tensor_engine_busy(1)
+        transpose_t0(0, 1, "SS")
         quantise_t0(0, 0)
-        transpose_t0(0, 1, "SV")
-        multiply_by_w(0, 0, "S")
+        reorder_w_codes()
+        keep_tensor_engine_busy(2)
         quantise_t0(0, 1)
-        multiply_by_w(0, 1, "V")
+        multiply_by_w(0, 0, "V")
+        multiply_by_w(0, 1, "S")
         multiply_by_w(0, 2, "S")
-        quantise_q(0, 0)
         multiply_by_w(0, 3, "V")
+        quantise_q(0, 0)
         transpose_t1(0, 0, "SS")
         quantise_q(0, 1)
+        keep_tensor_engine_busy(2)
         quantise_t1(0, 0)
         transpose_t0(0, 2, "SS")
-        keep_tensor_engine_busy(2)
-        half_scores(0, 0, "left0")
-        transpose_t0(0, 3, "SV")
+        transpose_t0(0, 3, "VS")
         quantise_t0(0, 2)
-        transpose_t1(0, 1, "SV")
-        keep_tensor_engine_busy(1)
-        multiply_by_w(0, 4, "S")
         quantise_t0(0, 3)
+        half_scores(0, 0, "left0", "SV")
+        transpose_t1(0, 1, "SS")
         quantise_t1(0, 1)
+        multiply_by_w(0, 4, "S")
         multiply_by_w(0, 5, "V")
-        half_scores(1, 0, "left1")
-        multiply_by_w(0, 6, "S")
+        multiply_by_w(0, 6, "V")
+        multiply_by_w(0, 7, "S")
+        half_scores(1, 0, "left1", "VS")
         quantise_q(0, 2)
-        multiply_by_w(0, 7, "V")
-        transpose_t1(0, 2, "S")
-        keep_tensor_engine_busy(3)
         quantise_q(0, 3)
-        half_scores(0, 1, "right0")
+        transpose_t1(0, 2, "S")
+        keep_tensor_engine_busy(1)
+        half_scores(0, 1, "right0", "VS")
         quantise_t1(0, 2)
-        half_scores(1, 1, "right1")
+        half_scores(1, 1, "right1", "VS")
         transpose_t1(0, 3, "S")
+        quantise_t1(0, 3)
 
         def rows_and_store(s, r0, count):
             result = results_of("%d_%d" % (s, r0), count, ROWS)
@@ -288,7 +289,6 @@ def tile_bilinear_kernel(tc, tensor0, tensor1, kernel_words, kernel_scales, bias
         last = results_of("0_6", 2, ROWS)
         transpose_t0(1, 0, "S")
         row_scores(0, 4, middle[:, 0, :])
-        quantise_t1(0, 3)
         quantise_t0(1, 0)
         row_scores(0, 5, middle[:, 1, :])
         store(0, 4, 2, whole, middle[:])

@@ -73,8 +73,9 @@ def tile_bilinear_kernel(tc, tensor0, tensor1, kernel_words, kernel_scales, bias
             rows = tensor0[s, BANK * half : BANK * (half + 1), :].rearrange("(p h) e -> p h e", h=HALF_FOLD)
             nc.sync.dma_start(out=t0_raw[s][:, half, h0 : h0 + count], in_=rows[:, h0 : h0 + count])
 
-        def load_t1(s):
-            nc.sync.dma_start(out=t1_raw[s][:], in_=tensor1[s].rearrange("(p r) d -> p r d", r=T1_FOLD))
+        def load_t1(s, r0, count):
+            rows = tensor1[s].rearrange("(p r) d -> p r d", r=T1_FOLD)
+            nc.sync.dma_start(out=t1_raw[s][:, r0 : r0 + count], in_=rows[:, r0 : r0 + count])
 
         def load_w_scales():
             for quadrant in range(4):
@@ -96,11 +97,12 @@ def tile_bilinear_kernel(tc, tensor0, tensor1, kernel_words, kernel_scales, bias
         load_t0(0, 0, UNIT_STEP, UNIT_STEP)
         load_w_scales()
         load_w_codes()
-        load_t1(0)
+        load_t1(0, 0, 4)
         load_t0(0, 1, 0, HALF_FOLD)
+        load_t1(0, 4, 4)
         for half in range(HALVES):
             load_t0(1, half, 0, HALF_FOLD)
-        load_t1(1)
+        load_t1(1, 0, T1_FOLD)
 
         def keep_tensor_engine_busy(count):
             unread = psum_sums.tile([P, BANK], F32, tag="sums")
@@ -218,10 +220,14 @@ def tile_bilinear_kernel(tc, tensor0, tensor1, kernel_words, kernel_scales, bias
             else:
                 nc.scalar.activation(out=out_half, in_=score_in_order, func=IDENTITY, bias=bias_f32[:, 0:1])
 
-        def store(s, r0, count, j_cols, values):
-            for b in range(COPIES):
-                rows = out[b, s].rearrange("(p r) j -> p r j", r=T1_FOLD)
-                nc.sync.dma_start(out=rows[:, r0 : r0 + count, j_cols], in_=values)
+        def store(s, r0, j_cols, values):
+            rows = out[:, s].rearrange("b (p r) j -> p b (r j)", r=T1_FOLD)
+            width = values.shape[1]
+            first = ROWS * r0 + j_cols.start
+            nc.sync.dma_start(
+                out=rows[:, :, first : first + width],
+                in_=values.unsqueeze(1).to_broadcast([P, COPIES, width]),
+            )
 
         def results_of(name, count, columns):
             return results.tile([P, count, columns], F32, name="result_" + name)
@@ -231,10 +237,11 @@ def tile_bilinear_kernel(tc, tensor0, tensor1, kernel_words, kernel_scales, bias
         whole = slice(0, ROWS)
 
         def half_scores(a, half, name, engines):
-            result = results_of(name, T1_STEP, BANK)
             for i, engine in enumerate(engines):
-                half_score(0, T1_STEP * a + i, half, result[:, i, :], engine)
-            store(0, T1_STEP * a, T1_STEP, (left, right)[half], result[:])
+                r = T1_STEP * a + i
+                result = results_of("%s_%d" % (name, i), 1, BANK)
+                half_score(0, r, half, result[:, 0, :], engine)
+                store(0, r, (left, right)[half], result[:, 0, :])
 
         def row_scores(s, r, result_row):
             half_score(s, r, 0, result_row[:, left], "V")
@@ -283,7 +290,7 @@ def tile_bilinear_kernel(tc, tensor0, tensor1, kernel_words, kernel_scales, bias
             result = results_of("%d_%d" % (s, r0), count, ROWS)
             for r in range(count):
                 row_scores(s, r0 + r, result[:, r, :])
-            store(s, r0, count, whole, result[:])
+            store(s, r0, whole, result[:].rearrange("p r j -> p (r j)"))
 
         middle = results_of("0_4", 2, ROWS)
         last = results_of("0_6", 2, ROWS)
@@ -291,7 +298,7 @@ def tile_bilinear_kernel(tc, tensor0, tensor1, kernel_words, kernel_scales, bias
         row_scores(0, 4, middle[:, 0, :])
         quantise_t0(1, 0)
         row_scores(0, 5, middle[:, 1, :])
-        store(0, 4, 2, whole, middle[:])
+        store(0, 4, whole, middle[:].rearrange("p r j -> p (r j)"))
         transpose_t0(1, 1, "S")
         keep_tensor_engine_busy(1)
         multiply_by_w(1, 0, "V")
@@ -309,7 +316,7 @@ def tile_bilinear_kernel(tc, tensor0, tensor1, kernel_words, kernel_scales, bias
         multiply_by_w(1, 4, "V")
         multiply_by_w(1, 5, "S")
         row_scores(0, 7, last[:, 1, :])
-        store(0, 6, 2, whole, last[:])
+        store(0, 6, whole, last[:].rearrange("p r j -> p (r j)"))
         transpose_t1(1, 0, "S")
         quantise_q(1, 2)
         quantise_t1(1, 0)
@@ -324,12 +331,12 @@ def tile_bilinear_kernel(tc, tensor0, tensor1, kernel_words, kernel_scales, bias
         row_scores(1, 0, first[:, 0, :])
         transpose_t1(1, 2, "S")
         row_scores(1, 1, first[:, 1, :])
-        store(1, 0, 2, whole, first[:])
+        store(1, 0, whole, first[:].rearrange("p r j -> p (r j)"))
         quantise_t1(1, 2)
         second = results_of("1_2", 2, ROWS)
         row_scores(1, 2, second[:, 0, :])
         transpose_t1(1, 3, "S")
         row_scores(1, 3, second[:, 1, :])
-        store(1, 2, 2, whole, second[:])
+        store(1, 2, whole, second[:].rearrange("p r j -> p (r j)"))
         quantise_t1(1, 3)
         rows_and_store(1, 4, 4)

@@ -69,9 +69,9 @@ def tile_bilinear_kernel(tc, tensor0, tensor1, kernel_words, kernel_scales, bias
         def step_cols(a):
             return slice(STEP_ROWS * a, STEP_ROWS * (a + 1))
 
-        def load_t0(s, half, h0, count):
-            rows = tensor0[s, BANK * half : BANK * (half + 1), :].rearrange("(p h) e -> p h e", h=HALF_FOLD)
-            nc.sync.dma_start(out=t0_raw[s][:, half, h0 : h0 + count], in_=rows[:, h0 : h0 + count])
+        def load_t0(s, halves, h0, count):
+            rows = tensor0[s].rearrange("(f p h) e -> p f h e", f=HALVES, h=HALF_FOLD)
+            nc.sync.dma_start(out=t0_raw[s][:, halves, h0 : h0 + count], in_=rows[:, halves, h0 : h0 + count])
 
         def load_t1(s, r0, count):
             rows = tensor1[s].rearrange("(p r) d -> p r d", r=T1_FOLD)
@@ -91,7 +91,7 @@ def tile_bilinear_kernel(tc, tensor0, tensor1, kernel_words, kernel_scales, bias
             )
 
         nc.vector.memset(w_scales_raw[:].bitcast(I32), 0)
-        nc.vector.memset(zeros[:], 0.0)
+        nc.vector.memset(zeros[:].bitcast(I32), 0)
         nc.vector.memset(table_warmer[:], 0.0)
         load_t0(0, 0, 0, UNIT_STEP)
         load_t0(0, 0, UNIT_STEP, UNIT_STEP)
@@ -100,8 +100,7 @@ def tile_bilinear_kernel(tc, tensor0, tensor1, kernel_words, kernel_scales, bias
         load_t1(0, 0, 4)
         load_t0(0, 1, 0, HALF_FOLD)
         load_t1(0, 4, 4)
-        for half in range(HALVES):
-            load_t0(1, half, 0, HALF_FOLD)
+        load_t0(1, slice(0, HALVES), 0, HALF_FOLD)
         load_t1(1, 0, T1_FOLD)
 
         def keep_tensor_engine_busy(count):
@@ -279,18 +278,12 @@ def tile_bilinear_kernel(tc, tensor0, tensor1, kernel_words, kernel_scales, bias
         quantise_q(0, 2)
         quantise_q(0, 3)
         transpose_t1(0, 2, "S")
+        transpose_t1(0, 3, "V")
         keep_tensor_engine_busy(1)
         half_scores(0, 1, "right0", "VS")
         quantise_t1(0, 2)
         half_scores(1, 1, "right1", "VS")
-        transpose_t1(0, 3, "S")
         quantise_t1(0, 3)
-
-        def rows_and_store(s, r0, count):
-            result = results_of("%d_%d" % (s, r0), count, ROWS)
-            for r in range(count):
-                row_scores(s, r0 + r, result[:, r, :])
-            store(s, r0, whole, result[:].rearrange("p r j -> p (r j)"))
 
         middle = results_of("0_4", 2, ROWS)
         last = results_of("0_6", 2, ROWS)
@@ -333,10 +326,11 @@ def tile_bilinear_kernel(tc, tensor0, tensor1, kernel_words, kernel_scales, bias
         row_scores(1, 1, first[:, 1, :])
         store(1, 0, whole, first[:].rearrange("p r j -> p (r j)"))
         quantise_t1(1, 2)
-        second = results_of("1_2", 2, ROWS)
-        row_scores(1, 2, second[:, 0, :])
+        rest = results_of("1_2", 6, ROWS)
+        row_scores(1, 2, rest[:, 0, :])
         transpose_t1(1, 3, "S")
-        row_scores(1, 3, second[:, 1, :])
-        store(1, 2, whole, second[:].rearrange("p r j -> p (r j)"))
+        row_scores(1, 3, rest[:, 1, :])
         quantise_t1(1, 3)
-        rows_and_store(1, 4, 4)
+        for r in range(4, T1_FOLD):
+            row_scores(1, r, rest[:, r - 2, :])
+        store(1, 2, whole, rest[:].rearrange("p r j -> p (r j)"))

@@ -90,8 +90,8 @@ def tile_bilinear_kernel(tc, tensor0, tensor1, kernel_words, kernel_scales, bias
                 in_=kernel_words[0].rearrange("p n t -> p (n t)").bitcast(I32),
             )
 
-        nc.vector.memset(w_scales_raw[:].bitcast(I32), 0)
         nc.vector.memset(zeros[:].bitcast(I32), 0)
+        nc.vector.memset(w_scales_raw[:].bitcast(I32), 0)
         nc.vector.memset(table_warmer[:], 0.0)
         load_t0(0, 0, 0, UNIT_STEP)
         load_t0(0, 0, UNIT_STEP, UNIT_STEP)
@@ -285,50 +285,47 @@ def tile_bilinear_kernel(tc, tensor0, tensor1, kernel_words, kernel_scales, bias
         half_scores(1, 1, "right1", "VS")
         quantise_t1(0, 3)
 
-        middle = results_of("0_4", 2, ROWS)
-        last = results_of("0_6", 2, ROWS)
-        transpose_t0(1, 0, "S")
-        row_scores(0, 4, middle[:, 0, :])
+        transpose_t0(1, 0, "SV")
+        transpose_t0(1, 1, "SV")
+        last = results_of("0_4", 4, ROWS)
+        row_scores(0, 4, last[:, 0, :])
+        row_scores(0, 5, last[:, 1, :])
         quantise_t0(1, 0)
-        row_scores(0, 5, middle[:, 1, :])
-        store(0, 4, whole, middle[:].rearrange("p r j -> p (r j)"))
-        transpose_t0(1, 1, "S")
-        keep_tensor_engine_busy(1)
-        multiply_by_w(1, 0, "V")
         quantise_t0(1, 1)
-        multiply_by_w(1, 1, "S")
+        row_scores(0, 6, last[:, 2, :])
+        row_scores(0, 7, last[:, 3, :])
+        store(0, 4, whole, last[:].rearrange("p r j -> p (r j)"))
+
         transpose_t0(1, 2, "S")
-        quantise_q(1, 0)
+        transpose_t0(1, 3, "S")
         quantise_t0(1, 2)
+        multiply_by_w(1, 0, "V")
+        multiply_by_w(1, 1, "S")
+        quantise_t0(1, 3)
         multiply_by_w(1, 2, "V")
         multiply_by_w(1, 3, "S")
-        row_scores(0, 6, last[:, 0, :])
-        transpose_t0(1, 3, "S")
+        transpose_t1(1, 0, "S")
+        transpose_t1(1, 1, "S")
+        quantise_q(1, 0)
         quantise_q(1, 1)
-        quantise_t0(1, 3)
+        quantise_t1(1, 0)
         multiply_by_w(1, 4, "V")
         multiply_by_w(1, 5, "S")
-        row_scores(0, 7, last[:, 1, :])
-        store(0, 6, whole, last[:].rearrange("p r j -> p (r j)"))
-        transpose_t1(1, 0, "S")
-        quantise_q(1, 2)
-        quantise_t1(1, 0)
         multiply_by_w(1, 6, "V")
         multiply_by_w(1, 7, "S")
-        transpose_t1(1, 1, "S")
-        keep_tensor_engine_busy(3)
-        quantise_q(1, 3)
         quantise_t1(1, 1)
-
+        transpose_t1(1, 2, "S")
+        quantise_q(1, 2)
+        quantise_q(1, 3)
+        keep_tensor_engine_busy(2)
+        transpose_t1(1, 3, "S")
+        quantise_t1(1, 2)
         first = results_of("1_0", 2, ROWS)
         row_scores(1, 0, first[:, 0, :])
-        transpose_t1(1, 2, "S")
         row_scores(1, 1, first[:, 1, :])
         store(1, 0, whole, first[:].rearrange("p r j -> p (r j)"))
-        quantise_t1(1, 2)
         rest = results_of("1_2", 6, ROWS)
         row_scores(1, 2, rest[:, 0, :])
-        transpose_t1(1, 3, "S")
         row_scores(1, 3, rest[:, 1, :])
         quantise_t1(1, 3)
         for r in range(4, T1_FOLD):

import concourse.mybir as mybir
from concourse.masks import make_identity

BF16 = mybir.dt.bfloat16
F32 = mybir.dt.float32
I32 = mybir.dt.int32
U32 = mybir.dt.uint32
U8 = mybir.dt.uint8
FP8X4 = mybir.dt.float8_e4m3fn_x4
IDENTITY = mybir.ActivationFunctionType.Identity

S = 2
COPIES = 2
ROWS = 1024
D = 512
P = 128
PACK = 4
BANK = 512

STEPS = 4
STEP_ROWS = ROWS // STEPS
HALVES = ROWS // BANK
HALF_FOLD = BANK // P
UNIT_STEP = STEP_ROWS // P
T1_FOLD = ROWS // P
T1_STEP = T1_FOLD // STEPS

WARM_UP = 6

FLOPS = 2 * S * ROWS * D * D + 2 * S * ROWS * ROWS * D


def tile_bilinear_kernel(tc, tensor0, tensor1, kernel_words, kernel_scales, bias, out):
    nc = tc.nc
    with (
        tc.tile_pool(name="constants", bufs=1) as constants,
        tc.tile_pool(name="inputs", bufs=1) as inputs,
        tc.tile_pool(name="operands", bufs=1) as operands,
        tc.tile_pool(name="results", bufs=1) as results,
        tc.psum_pool(name="psum_transposed", bufs=4) as psum_transposed,
        tc.psum_pool(name="psum_sums", bufs=4) as psum_sums,
        tc.manual_schedule(),
    ):
        ident_f32 = constants.tile([P, P], F32)
        bias_bf16 = constants.tile([P, 1], BF16)
        bias_f32 = constants.tile([P, 1], F32)
        table_warmer = constants.tile([P, 1], F32)
        zeros = constants.tile([P, BANK], BF16)
        w_codes_raw = constants.tile([P, D], U32, align_bytes=64)
        w_scales_raw = constants.tile([P, D], U8, align_bytes=64)
        w_codes = constants.tile([P, D], U32, align_bytes=64)
        w_scales = constants.tile([P, D], U8, align_bytes=64)
        t0_raw = [inputs.tile([P, HALVES, HALF_FOLD, D], BF16, name="t0_raw%d" % s) for s in range(S)]
        t1_raw = [inputs.tile([P, T1_FOLD, D], BF16, name="t1_raw%d" % s) for s in range(S)]

        t0_grouped = operands.tile([P, ROWS, PACK], BF16, align_bytes=64)
        q_grouped = operands.tile([P, ROWS, PACK], BF16, align_bytes=64)
        t1_grouped = operands.tile([P, ROWS, PACK], BF16, align_bytes=64)

        def mx_operand(name):
            codes = [operands.tile([P, ROWS], U32, name="%s_codes%d" % (name, s), align_bytes=64) for s in range(S)]
            scales = [operands.tile([P, ROWS], U8, name="%s_scales%d" % (name, s), align_bytes=64) for s in range(S)]
            return codes, scales

        t0_codes, t0_scales = mx_operand("t0")
        q_codes, q_scales = mx_operand("q")
        t1_codes, t1_scales = mx_operand("t1")

        def step_cols(a):
            return slice(STEP_ROWS * a, STEP_ROWS * (a + 1))

        def load_t0(s, halves, h0, count):
            rows = tensor0[s].rearrange("(f p h) e -> p f h e", f=HALVES, h=HALF_FOLD)
            nc.sync.dma_start(out=t0_raw[s][:, halves, h0 : h0 + count], in_=rows[:, halves, h0 : h0 + count])

        def load_t1(s, r0, count):
            rows = tensor1[s].rearrange("(p r) d -> p r d", r=T1_FOLD)
            nc.sync.dma_start(out=t1_raw[s][:, r0 : r0 + count], in_=rows[:, r0 : r0 + count])

        def load_w_scales():
            for quadrant in range(4):
                nc.sync.dma_start(
                    out=w_scales_raw[32 * quadrant : 32 * quadrant + 4, :].bitcast(I32),
                    in_=kernel_scales[0, 4 * quadrant : 4 * quadrant + 4, :].bitcast(I32),
                )

        def load_w_codes():
            nc.sync.dma_start(
                out=w_codes_raw[:].bitcast(I32),
                in_=kernel_words[0].rearrange("p n t -> p (n t)").bitcast(I32),
            )

        nc.vector.memset(zeros[:].bitcast(I32), 0)
        nc.vector.memset(w_scales_raw[:].bitcast(I32), 0)
        nc.vector.memset(table_warmer[:], 0.0)
        load_t0(0, 0, 0, UNIT_STEP)
        load_t0(0, 0, UNIT_STEP, UNIT_STEP)
        load_w_scales()
        load_w_codes()
        load_t1(0, 0, 4)
        load_t0(0, 1, 0, HALF_FOLD)
        load_t1(0, 4, 4)
        load_t0(1, slice(0, HALVES), 0, HALF_FOLD)
        load_t1(1, 0, T1_FOLD)

        def keep_tensor_engine_busy(count):
            unread = psum_sums.tile([P, BANK], F32, tag="sums")
            for i in range(count):
                nc.tensor.matmul(out=unread[:], lhsT=zeros[:, 0:P], rhs=zeros[:], start=(i == 0), stop=(i == count - 1))

        keep_tensor_engine_busy(WARM_UP)

        nc.scalar.activation(out=table_warmer[:], in_=table_warmer[:], func=IDENTITY)

        nc.gpsimd.dma_start(out=bias_bf16[:], in_=bias.partition_broadcast(P))
        make_identity(nc, ident_f32[:])
        nc.gpsimd.tensor_copy(out=bias_f32[:], in_=bias_bf16[:])

        def reorder(out, in_):
            nc.vector.tensor_copy(
                out=out.rearrange("p (t m) -> p t m", t=PACK), in_=in_.rearrange("p (m t) -> p t m", t=PACK)
            )

        def reorder_w_scales():
            reorder(w_scales[:], w_scales_raw[:])

        def reorder_w_codes():
            reorder(w_codes[:].bitcast(I32), w_codes_raw[:].bitcast(I32))

        def copy_out(engine, out, in_):
            if engine == "V":
                nc.vector.tensor_copy(out=out, in_=in_)
            else:
                nc.scalar.copy(out=out, in_=in_)

        def unit_cols(u):
            return slice(P * u, P * (u + 1))

        def transpose_words(columns, words, count, engine):
            turned = psum_transposed.tile([P, count, 2, P], F32, tag="transposed")
            for i in range(count):
                for u in range(2):
                    nc.tensor.transpose(turned[:, i, u, :], words[:, i, u : D // 2 : 2], ident_f32[:])
            copy_out(
                engine,
                columns.bitcast(F32).rearrange("p (i c) u -> p i c u", i=count),
                turned[:].rearrange("p i u c -> p i c u"),
            )

        def transpose_step(raw, grouped, a, engines):
            words = raw.bitcast(F32)
            count = UNIT_STEP // len(engines)
            for i, engine in enumerate(engines):
                u = UNIT_STEP * a + count * i
                transpose_words(grouped[:, P * u : P * (u + count), :], words[:, u : u + count, :], count, engine)

        def transpose_t0(s, a, engines):
            transpose_step(t0_raw[s][:].rearrange("p f h e -> p (f h) e"), t0_grouped, a, engines)

        def quantise_t0(s, a):
            nc.vector.quantize_mx(
                out=t0_codes[s][:, step_cols(a)].bitcast(FP8X4),
                scales=t0_scales[s][:, step_cols(a)],
                in_=t0_grouped[:, step_cols(a), :].rearrange("p j t -> p (j t)"),
            )

        def multiply_by_w(s, u, engine):
            j_cols = unit_cols(u)
            q_t = psum_sums.tile([P, PACK, P], F32, tag="sums")
            for t in range(PACK):
                d_cols = slice(P * t, P * (t + 1))
                nc.tensor.matmul_mx(
                    out=q_t[:, t, :],
                    lhsT=w_codes[:, d_cols].bitcast(FP8X4),
                    lhsT_scale=w_scales[:, d_cols],
                    rhs=t0_codes[s][:, j_cols].bitcast(FP8X4),
                    rhs_scale=t0_scales[s][:, j_cols],
                    start=True,
                    stop=True,
                )
            copy_out(engine, q_grouped[:, j_cols, :], q_t[:].rearrange("p t j -> p j t"))

        def quantise_q(s, a):
            nc.vector.quantize_mx(
                out=q_codes[s][:, step_cols(a)].bitcast(FP8X4),
                scales=q_scales[s][:, step_cols(a)],
                in_=q_grouped[:, step_cols(a), :].rearrange("p j t -> p (j t)"),
            )

        def transpose_t1(s, a, engines):
            transpose_step(t1_raw[s][:], t1_grouped, a, engines)

        def quantise_t1(s, a):
            nc.vector.quantize_mx(
                out=t1_codes[s][:, step_cols(a)].bitcast(FP8X4),
                scales=t1_scales[s][:, step_cols(a)],
                in_=t1_grouped[:, step_cols(a), :].rearrange("p i t -> p (i t)"),
            )

        def half_score(s, r, half, result, engine):
            i_cols = unit_cols(r)
            j_cols = slice(BANK * half, BANK * (half + 1))
            score = psum_sums.tile([P, HALF_FOLD, P], F32, tag="sums")
            nc.tensor.matmul_mx(
                out=score[:].rearrange("p h c -> p (h c)"),
                lhsT=t1_codes[s][:, i_cols].bitcast(FP8X4),
                lhsT_scale=t1_scales[s][:, i_cols],
                rhs=q_codes[s][:, j_cols].bitcast(FP8X4),
                rhs_scale=q_scales[s][:, j_cols],
                start=True,
                stop=True,
            )
            out_half = result.rearrange("p (c h) -> p c h", h=HALF_FOLD)
            score_in_order = score[:].rearrange("p h c -> p c h")
            if engine == "V":
                nc.vector.tensor_scalar(
                    out=out_half, in0=score_in_order, scalar1=bias_f32[:, 0:1], scalar2=None, op0=mybir.AluOpType.add
                )
            else:
                nc.scalar.activation(out=out_half, in_=score_in_order, func=IDENTITY, bias=bias_f32[:, 0:1])

        def store(s, r0, j_cols, values):
            rows = out[:, s].rearrange("b (p r) j -> p b (r j)", r=T1_FOLD)
            width = values.shape[1]
            first = ROWS * r0 + j_cols.start
            nc.sync.dma_start(
                out=rows[:, :, first : first + width],
                in_=values.unsqueeze(1).to_broadcast([P, COPIES, width]),
            )

        def results_of(name, count, columns):
            return results.tile([P, count, columns], F32, name="result_" + name)

        left = slice(0, BANK)
        right = slice(BANK, ROWS)
        whole = slice(0, ROWS)

        def half_scores(a, half, name, engines):
            for i, engine in enumerate(engines):
                r = T1_STEP * a + i
                result = results_of("%s_%d" % (name, i), 1, BANK)
                half_score(0, r, half, result[:, 0, :], engine)
                store(0, r, (left, right)[half], result[:, 0, :])

        def row_scores(s, r, result_row):
            half_score(s, r, 0, result_row[:, left], "V")
            half_score(s, r, 1, result_row[:, right], "S")

        transpose_t0(0, 0, "SS")
        reorder_w_scales()
        keep_tensor_engine_busy(1)
        transpose_t0(0, 1, "SS")
        quantise_t0(0, 0)
        reorder_w_codes()
        keep_tensor_engine_busy(2)
        quantise_t0(0, 1)
        multiply_by_w(0, 0, "V")
        multiply_by_w(0, 1, "S")
        multiply_by_w(0, 2, "S")
        multiply_by_w(0, 3, "V")
        quantise_q(0, 0)
        transpose_t1(0, 0, "SS")
        quantise_q(0, 1)
        keep_tensor_engine_busy(2)
        quantise_t1(0, 0)
        transpose_t0(0, 2, "SS")
        transpose_t0(0, 3, "VS")
        quantise_t0(0, 2)
        quantise_t0(0, 3)
        half_scores(0, 0, "left0", "SV")
        transpose_t1(0, 1, "SS")
        quantise_t1(0, 1)
        multiply_by_w(0, 4, "S")
        multiply_by_w(0, 5, "V")
        multiply_by_w(0, 6, "V")
        multiply_by_w(0, 7, "S")
        half_scores(1, 0, "left1", "VS")
        quantise_q(0, 2)
        quantise_q(0, 3)
        transpose_t1(0, 2, "S")
        transpose_t1(0, 3, "V")
        keep_tensor_engine_busy(1)
        half_scores(0, 1, "right0", "VS")
        quantise_t1(0, 2)
        half_scores(1, 1, "right1", "VS")
        quantise_t1(0, 3)

        transpose_t0(1, 0, "SV")
        transpose_t0(1, 1, "SV")
        last = results_of("0_4", 4, ROWS)
        row_scores(0, 4, last[:, 0, :])
        row_scores(0, 5, last[:, 1, :])
        quantise_t0(1, 0)
        quantise_t0(1, 1)
        row_scores(0, 6, last[:, 2, :])
        row_scores(0, 7, last[:, 3, :])
        store(0, 4, whole, last[:].rearrange("p r j -> p (r j)"))

        transpose_t0(1, 2, "S")
        transpose_t0(1, 3, "S")
        quantise_t0(1, 2)
        multiply_by_w(1, 0, "V")
        multiply_by_w(1, 1, "S")
        quantise_t0(1, 3)
        multiply_by_w(1, 2, "V")
        multiply_by_w(1, 3, "S")
        transpose_t1(1, 0, "S")
        transpose_t1(1, 1, "S")
        quantise_q(1, 0)
        quantise_q(1, 1)
        quantise_t1(1, 0)
        multiply_by_w(1, 4, "V")
        multiply_by_w(1, 5, "S")
        multiply_by_w(1, 6, "V")
        multiply_by_w(1, 7, "S")
        quantise_t1(1, 1)
        transpose_t1(1, 2, "S")
        quantise_q(1, 2)
        quantise_q(1, 3)
        keep_tensor_engine_busy(2)
        transpose_t1(1, 3, "S")
        quantise_t1(1, 2)
        first = results_of("1_0", 2, ROWS)
        row_scores(1, 0, first[:, 0, :])
        row_scores(1, 1, first[:, 1, :])
        store(1, 0, whole, first[:].rearrange("p r j -> p (r j)"))
        rest = results_of("1_2", 6, ROWS)
        row_scores(1, 2, rest[:, 0, :])
        row_scores(1, 3, rest[:, 1, :])
        quantise_t1(1, 3)
        for r in range(4, T1_FOLD):
            row_scores(1, r, rest[:, r - 2, :])
        store(1, 2, whole, rest[:].rearrange("p r j -> p (r j)"))
